import numpy as np
import ml_dtypes


BF16 = ml_dtypes.bfloat16


def bf(x):
    return np.asarray(x, np.float32).astype(BF16)


def f64(x):
    return np.asarray(x).astype(np.float64)


E2M1 = np.array([0.0, 0.5, 1.0, 1.5, 2.0, 3.0, 4.0, 6.0, -0.0, -0.5, -1.0, -1.5, -2.0, -3.0, -4.0, -6.0])


def pack_weight(w, fmt):
    k, n = w.shape
    w = f64(bf(w)).reshape(k // 32, 32, n)
    amax = np.abs(w).max(1)
    if fmt == "e4m3":
        byte = np.frexp(amax)[1] - 1 + 127 - 7
    else:
        mant, ex = np.frexp(amax / 6.0)
        byte = np.where(mant > 0.5, ex, ex - 1) + 127
    byte = np.clip(np.where(amax > 0, byte, 1), 1, 254)
    scaled = (w * np.exp2(127.0 - byte)[:, None, :]).reshape(k, n).astype(np.float32)
    by_word = np.ascontiguousarray(scaled.reshape(k // 512, 128, 4, n).transpose(0, 1, 3, 2))
    if fmt == "e4m3":
        words = by_word.astype(ml_dtypes.float8_e4m3fn).view(np.uint8)
    else:
        c = by_word.astype(ml_dtypes.float4_e2m1fn).view(np.uint8) & 0xF
        words = c[..., 0::2] | (c[..., 1::2] << 4)
    return np.ascontiguousarray(words), np.ascontiguousarray(byte.astype(np.uint8).reshape(k // 512, 16, n))


def unpack_weight(words, scales, fmt):
    g, p, n, _ = words.shape
    if fmt == "e4m3":
        vals = np.ascontiguousarray(words).view(ml_dtypes.float8_e4m3fn).astype(np.float64)
    else:
        nib = np.empty((g, p, n, 4), np.uint8)
        nib[..., 0::2] = words & 0xF
        nib[..., 1::2] = words >> 4
        vals = E2M1[nib]
    vals = vals * np.repeat(np.exp2(scales.astype(np.float64) - 127.0), 8, axis=1)[..., None]
    return vals.transpose(0, 1, 3, 2).reshape(g * 512, n)

def pack4(w):
    words, scales = pack_weight(w, "e2m1")
    return words.reshape(words.shape[0], 128, -1), scales


def unpack4(words, scales):
    return unpack_weight(words.reshape(words.shape[0], 128, -1, 2), scales, "e2m1")


def kspread(k):
    return np.exp2(np.repeat(np.random.randint(-6, 7, k // 32), 32).astype(np.float64))


B, T, C, H, G = 2, 256, 4096, 16, 16
HS = C // H
TG = T // G
THETA = 10000.0


def apply_rope(t, cos, sin):
    tp = t.reshape(B, T, H, HS // 2, 2)
    a, b = tp[..., 0], tp[..., 1]
    c = cos[None, :, None, :]
    s = sin[None, :, None, :]
    return np.stack([a * c - b * s, a * s + b * c], axis=-1).reshape(B, T, H, HS)


def grp(t):
    return t.reshape(B, G, TG, H, HS).transpose(0, 3, 1, 2, 4)


def with_summary(t):
    return np.concatenate([t, t.mean(axis=3, keepdims=True)], axis=3)


def setup_inputs():
    s = kspread(C)
    x = np.random.standard_normal((B, T, C)) * 0.7 + np.random.standard_normal((B, 1, C)) * 0.7
    w = np.random.standard_normal((3 * C, C)) / np.sqrt(C)
    ang = np.arange(T)[:, None] / THETA ** (np.arange(0, HS, 2) / HS)[None, :]
    words, scales = pack4((w / s[None, :]).T)
    x_words, x_scales = pack4((x * s).reshape(B * T, C).T)
    return {"x_words": x_words, "x_scales": x_scales, "w_attn_words": words, "w_attn_scales": scales, "freqs_cos": bf(np.cos(ang)), "freqs_sin": bf(np.sin(ang))}


def reference(x_words, x_scales, w_attn_words, w_attn_scales, freqs_cos, freqs_sin):
    cos, sin = f64(freqs_cos), f64(freqs_sin)
    qkv = unpack4(x_words, x_scales).T.reshape(B, T, C) @ unpack4(w_attn_words, w_attn_scales)
    q, k, v = np.split(qkv, 3, axis=2)
    q = apply_rope(q.reshape(B, T, H, HS), cos, sin).reshape(B, T, C)
    k = apply_rope(k.reshape(B, T, H, HS), cos, sin).reshape(B, T, C)
    q, k, v = grp(q), grp(k), grp(v)
    return with_summary(q), with_summary(k), with_summary(v)

@@ -1,0 +1,341 @@
+from contextlib import ExitStack
+
+import concourse.mybir as mybir
+
+B, T, C, H = 2, 256, 4096, 16
+G = 16
+TG = T // G
+HS = C // H
+TOK = B * T
+
+F32 = mybir.dt.float32
+BF16 = mybir.dt.bfloat16
+I32 = mybir.dt.int32
+U8 = mybir.dt.uint8
+FP4X4 = mybir.dt.float4_e2m1fn_x4
+ADD = mybir.AluOpType.add
+MULT = mybir.AluOpType.mult
+COPY = mybir.ActivationFunctionType.Copy
+AXIS_X = mybir.AxisListType.X
+
+FLOPS = 2 * TOK * C * 3 * C
+
+P = 128
+PASSES = C // 512
+J = TOK // P
+NB = 512
+CHUNK = 1024
+NBLK = CHUNK // NB
+HC = CHUNK // HS
+HB = NB // HS
+
+
+def tile_causalselfattention2_pa_kernel(
+    tc, x_words, x_scales, w_words, w_scales, freqs_cos, freqs_sin, out_q, out_k, out_v
+):
+    nc = tc.nc
+    outs = [out_q, out_k, out_v]
+    order = [(part, quarter) for quarter in range(C // CHUNK) for part in range(3)]
+
+    with ExitStack() as ctx:
+        keep = ctx.enter_context(tc.tile_pool(name="keep", bufs=1))
+        codes = ctx.enter_context(tc.tile_pool(name="codes", bufs=3))
+        rows = ctx.enter_context(tc.tile_pool(name="rows", bufs=3))
+        crossed = ctx.enter_context(tc.tile_pool(name="crossed", bufs=3))
+        sums = ctx.enter_context(tc.tile_pool(name="sums", bufs=2))
+        psum = ctx.enter_context(tc.psum_pool(name="psum", bufs=8))
+        ctx.enter_context(tc.manual_schedule())
+
+        x_raw = keep.tile([P, PASSES, 2 * TOK], U8, align_bytes=64, name="x_raw")
+        xs_raw = keep.tile([P, PASSES, TOK], U8, align_bytes=64, name="xs_raw")
+        x_codes = keep.tile([P, PASSES, J, 2 * P], U8, align_bytes=64, name="x_codes")
+        x_planes = keep.tile([P, PASSES, J, P], U8, align_bytes=64, name="x_planes")
+        w_planes = [
+            keep.tile([P, PASSES, CHUNK], U8, align_bytes=64, name="w_planes%d" % i) for i in range(3)
+        ]
+        cs_raw = keep.tile([P, 2, J, HS // 2], BF16, name="cs_raw")
+        cos2 = keep.tile([P, J, HB, HS // 2, 2], BF16, name="cos2")
+        sin2 = keep.tile([P, J, HB, HS // 2, 2], BF16, name="sin2")
+
+        w_tiles = {}
+
+        def col0(s):
+            part, quarter = order[s]
+            return part * C + quarter * CHUNK
+
+        def load_w_codes(s, g0, g1):
+            if s not in w_tiles:
+                w_tiles[s] = codes.tile([P, PASSES, 2 * CHUNK], U8, align_bytes=64, name="w_codes")
+            c = col0(s)
+            nc.sync.dma_start(
+                out=w_tiles[s][:, g0:g1, :],
+                in_=w_words[g0:g1, :, 2 * c : 2 * (c + CHUNK)].rearrange("g p n -> p g n"),
+            )
+
+        def load_w_scales(s):
+            c = col0(s)
+            for r in range(4):
+                nc.sync.dma_start(
+                    out=w_planes[s % 3][r:P:32, :, :].bitcast(I32),
+                    in_=w_scales[:, r:16:4, c : c + CHUNK].rearrange("g q n -> q g n").bitcast(I32),
+                )
+
+        def load_x_codes(g0, g1):
+            nc.sync.dma_start(
+                out=x_raw[:, g0:g1, :], in_=x_words[g0:g1].rearrange("g p n -> p g n")
+            )
+
+        nc.vector.memset(xs_raw[:].bitcast(I32), 0)
+        nc.gpsimd.memset(w_planes[0][:].bitcast(I32), 0)
+        load_x_codes(0, 1)
+        load_w_codes(0, 0, 1)
+        for q in range(4):
+            nc.sync.dma_start(
+                out=xs_raw[32 * q : 32 * q + 4, :, :].bitcast(I32),
+                in_=x_scales[:, 4 * q : 4 * q + 4, :].rearrange("g r n -> r g n").bitcast(I32),
+            )
+        load_w_scales(0)
+        load_x_codes(1, 2)
+        load_w_codes(0, 1, 2)
+        load_x_codes(2, 4)
+        load_w_codes(0, 2, 4)
+        load_x_codes(4, 8)
+        load_w_codes(0, 4, 8)
+        for half in range(2):
+            for i, f in enumerate((freqs_cos, freqs_sin)):
+                nc.gpsimd.dma_start(
+                    out=cs_raw[64 * half : 64 * half + 64, i, :, :],
+                    in_=f.rearrange("(p j) i -> p j i", j=J),
+                )
+        nc.gpsimd.memset(w_planes[1][:].bitcast(I32), 0)
+        nc.gpsimd.memset(w_planes[2][:].bitcast(I32), 0)
+
+        for h in range(HB):
+            for e in range(2):
+                nc.scalar.activation(out=cos2[:, :, h, :, e], in_=cs_raw[:, 0], func=COPY)
+                nc.scalar.activation(
+                    out=sin2[:, :, h, :, e], in_=cs_raw[:, 1], func=COPY, scale=1.0 - 2.0 * e
+                )
+
+        def permute_x(g):
+            nc.vector.tensor_copy(
+                out=x_codes[:, g].rearrange("p j (m b) -> p j m b", b=2),
+                in_=x_raw[:, g].rearrange("p (m j b) -> p j m b", j=J, b=2),
+            )
+
+        def permute_x_scales(g):
+            nc.vector.tensor_copy(
+                out=x_planes[:, g], in_=xs_raw[:, g].rearrange("p (m j) -> p j m", j=J)
+            )
+
+        for g in range(PASSES):
+            permute_x(g)
+            permute_x_scales(g)
+
+        pending = []
+
+        def pop():
+            if pending:
+                pending.pop(0)()
+
+        def store_rows(queue, s, r_tile, h, j0, j1):
+            part, quarter = order[s]
+            for b in range(B):
+                queue.dma_start(
+                    out=outs[part][b, quarter * HC + h, :, 0:TG, :].rearrange(
+                        "g (r j) c -> g r (j c)", j=J
+                    )[:, :, j0 * HS : j1 * HS],
+                    in_=r_tile[64 * b : 64 * b + 64, h, j0:j1, :].rearrange("p j c -> p (j c)"),
+                )
+
+        def store_means(queue, s, z):
+            part, quarter = order[s]
+            for q in range(4):
+                b, g0 = q // 2, 8 * (q % 2)
+                queue.dma_start(
+                    out=outs[part][b, quarter * HC : quarter * HC + HC, g0 : g0 + 8, TG, :],
+                    in_=z[32 * q : 32 * q + 32, :],
+                )
+
+        def make_add(s, r_tile, m_tile, blk):
+            def run():
+                r = r_tile[:, HB * blk : HB * blk + HB].rearrange("p h j (i e) -> p (h j i) e", e=2)
+                m = m_tile[:].rearrange("p h j (i e) -> p (h j i) e", e=2)
+                nc.vector.tensor_tensor(out=r, in0=r, in1=m[:, :, ::-1], op=ADD)
+                for h in range(HB * blk, HB * blk + HB):
+                    store_rows(nc.gpsimd, s, r_tile, h, 0, J)
+
+            return run
+
+        def push_mean(s, r_tile):
+            state = {}
+
+            def sum_a():
+                t = sums.tile([P, HC, 2 * HS], F32, name="pair_sums")
+                state["t"] = t
+                r = r_tile[:].rearrange("p h j c -> p h (j c)")
+                nc.vector.tensor_tensor(
+                    out=t[:], in0=r[:, :, 0 : 2 * HS], in1=r[:, :, 2 * HS : 4 * HS], op=ADD
+                )
+
+            def sum_b():
+                u = sums.tile([P, CHUNK], F32, align_bytes=64, name="four_sums")
+                t = state["t"]
+                state["u"] = u
+                nc.vector.tensor_tensor(
+                    out=u[:].rearrange("p (h c) -> p h c", h=HC),
+                    in0=t[:, :, 0:HS],
+                    in1=t[:, :, HS : 2 * HS],
+                    op=ADD,
+                )
+
+            def turn():
+                v = sums.tile([P, CHUNK], F32, align_bytes=64, name="turned")
+                nc.vector.transpose(out=v[:], in_=state["u"][:])
+                state["v"] = v
+
+            def reduce():
+                w = sums.tile([P, HS], F32, align_bytes=64, name="group_sums")
+                nc.vector.tensor_reduce(
+                    out=w[:].rearrange("p (m h g) -> p h m g", h=HC, g=8),
+                    in_=state["v"][:].rearrange("p (h m g r) -> p h m g r", h=HC, g=8, r=4),
+                    axis=AXIS_X,
+                    op=ADD,
+                )
+                state["w"] = w
+
+            def turn_back():
+                y = sums.tile([P, HS], F32, align_bytes=64, name="turned_back")
+                z = sums.tile([P, HS], F32, name="means")
+                nc.vector.transpose(out=y[:], in_=state["w"][:])
+                nc.scalar.activation(out=z[:], in_=y[:], func=COPY, scale=1.0 / TG)
+                store_means(nc.scalar, s, z)
+
+            pending.extend([sum_a, sum_b, turn, reduce, turn_back])
+
+        def one_pass(acc, s, g, c0, c1, j):
+            nc.tensor.matmul_mx(
+                out=acc[:, 0 : c1 - c0],
+                lhsT=x_codes[:, g, j, :].bitcast(FP4X4),
+                lhsT_scale=x_planes[:, g, j, :],
+                rhs=w_tiles[s][:, g, 2 * c0 : 2 * c1].bitcast(FP4X4),
+                rhs_scale=w_planes[s % 3][:, g, c0:c1],
+                start=(g == 0),
+                stop=(g == PASSES - 1),
+            )
+
+        def drain(s, acc, r_tile, m_tile, blk, j):
+            bank = acc[:].rearrange("p (h c) -> p h c", h=HB)
+            out = r_tile[:, HB * blk : HB * blk + HB, j, :]
+            if order[s][0] == 2:
+                nc.scalar.copy(out=out, in_=bank)
+            else:
+                nc.vector.tensor_tensor(
+                    out=out, in0=bank, in1=cos2[:, j].rearrange("p h i e -> p h (i e)"), op=MULT
+                )
+                nc.vector.tensor_tensor(
+                    out=m_tile[:, :, j, :],
+                    in0=bank,
+                    in1=sin2[:, j].rearrange("p h i e -> p h (i e)"),
+                    op=MULT,
+                )
+            pop()
+
+        def load_chunk(s):
+            if s < len(order):
+                load_w_scales(s)
+                load_w_codes(s, 0, 4)
+                load_w_codes(s, 4, 8)
+
+        load_chunk(1)
+        last = len(order) - 1
+        for s in range(last):
+            load_chunk(s + 2)
+            rotated = order[s][0] < 2
+            r_tile = rows.tile([P, HC, J, HS], F32, name="r_tile")
+            accs = {}
+            if s == 0:
+                for g in range(PASSES):
+                    for blk in range(NBLK):
+                        for j in range(J):
+                            if g == 0:
+                                accs[blk, j] = psum.tile([P, NB], F32, name="acc")
+                            one_pass(accs[blk, j], s, g, blk * NB, blk * NB + NB, j)
+            for blk in range(NBLK):
+                m_tile = crossed.tile([P, HB, J, HS], F32, name="m_tile") if rotated else None
+                for j in range(J):
+                    if s > 0:
+                        accs[blk, j] = psum.tile([P, NB], F32, name="acc")
+                        for g in range(PASSES):
+                            one_pass(accs[blk, j], s, g, blk * NB, blk * NB + NB, j)
+                    drain(s, accs[blk, j], r_tile, m_tile, blk, j)
+                if rotated:
+                    pending.append(make_add(s, r_tile, m_tile, blk))
+                else:
+                    for h in range(HB * blk, HB * blk + HB):
+                        store_rows(nc.gpsimd, s, r_tile, h, 0, J)
+            push_mean(s, r_tile)
+
+        s = last
+        r_tile = rows.tile([P, HC, J, HS], F32, name="r_tile")
+        w = sums.tile([P, HS], F32, align_bytes=64, name="group_sums")
+
+        def turn_and_reduce(u, h0, h1):
+            v = sums.tile([P, CHUNK], F32, align_bytes=64, name="turned")
+            n = (h1 - h0) * HS
+            nc.vector.transpose(out=v[:, 0:n], in_=u)
+            nc.vector.tensor_reduce(
+                out=w[:].rearrange("p (m h g) -> p h m g", h=HC, g=8)[:, h0:h1],
+                in_=v[:, 0:n].rearrange("p (h m g r) -> p h m g r", h=h1 - h0, g=8, r=4),
+                axis=AXIS_X,
+                op=ADD,
+            )
+
+        def first_block_sums():
+            t = sums.tile([P, HC, 2 * HS], F32, name="pair_sums")
+            r = r_tile[:, 0:HB].rearrange("p h j c -> p h (j c)")
+            nc.vector.tensor_tensor(
+                out=t[:, 0:HB], in0=r[:, :, 0 : 2 * HS], in1=r[:, :, 2 * HS : 4 * HS], op=ADD
+            )
+            u = sums.tile([P, CHUNK], F32, align_bytes=64, name="four_sums")
+            nc.vector.tensor_tensor(
+                out=u[:, 0:NB].rearrange("p (h c) -> p h c", h=HB),
+                in0=t[:, 0:HB, 0:HS],
+                in1=t[:, 0:HB, HS : 2 * HS],
+                op=ADD,
+            )
+            nc.scalar.activation(out=u[:, NB : 2 * NB], in_=u[:, 0:NB], func=COPY, scale=1.0 / TG)
+            turn_and_reduce(u[:, NB : 2 * NB], 0, HB)
+
+        for j in range(J):
+            acc = psum.tile([P, NB], F32, name="acc")
+            for g in range(PASSES):
+                one_pass(acc, s, g, 0, NB, j)
+            drain(s, acc, r_tile, None, 0, j)
+            pop()
+        for h in range(HB):
+            store_rows(nc.sync, s, r_tile, h, 0, J)
+        while pending:
+            pop()
+        first_block_sums()
+        for h in range(HB, HC):
+            parts = sums.tile([P, J, HS], F32, align_bytes=64, name="parts")
+            for j in range(J):
+                acc = psum.tile([P, NB], F32, name="acc")
+                for g in range(PASSES):
+                    one_pass(acc, s, g, h * HS, h * HS + HS, j)
+                bank = acc[:, 0:HS]
+                if j == 0:
+                    nc.scalar.activation(out=parts[:, 0], in_=bank, func=COPY, scale=1.0 / TG)
+                else:
+                    nc.vector.scalar_tensor_tensor(
+                        out=parts[:, j], in0=bank, scalar=1.0 / TG, in1=parts[:, j - 1], op0=MULT, op1=ADD
+                    )
+                nc.scalar.copy(out=r_tile[:, h, j, :], in_=bank)
+                if j == J - 2:
+                    store_rows(nc.sync, s, r_tile, h, 0, J - 1)
+            turn_and_reduce(parts[:, J - 1], h, h + 1)
+            store_rows(nc.sync, s, r_tile, h, J - 1, J)
+        y = sums.tile([P, HS], F32, align_bytes=64, name="turned_back")
+        nc.vector.transpose(out=y[:], in_=w[:])
+        store_means(nc.scalar, s, y)

@@ -148,13 +148,27 @@ def tile_causalselfattention2_pa_kernel(
                     in_=r_tile[64 * b : 64 * b + 64, h, j0:j1, :].rearrange("p j c -> p (j c)"),
                 )
 
-        def store_means(queue, s, z):
+        def head_means(queue, s, u, h):
             part, quarter = order[s]
+            v = sums.tile([P, HS], F32, align_bytes=64, name="turned")
+            w = sums.tile([P, HS // 4], F32, align_bytes=64, name="last_sums")
+            y = sums.tile([P, HS // 4], F32, align_bytes=64, name="turned_back")
+            nc.vector.transpose(out=v[:], in_=u)
+            nc.vector.tensor_reduce(
+                out=w[:].rearrange("p (m x g) -> p x m g", x=4, g=8),
+                in_=v[:].rearrange("p (x m g r) -> p x m g r", x=4, g=8, r=4),
+                axis=AXIS_X,
+                op=ADD,
+            )
+            for m in range(2):
+                nc.vector.transpose(out=y[:, 32 * m : 32 * m + 32], in_=w[:, 32 * m : 32 * m + 32])
             for q in range(4):
                 b, g0 = q // 2, 8 * (q % 2)
                 queue.dma_start(
-                    out=outs[part][b, quarter * HC : quarter * HC + HC, g0 : g0 + 8, TG, :],
-                    in_=z[32 * q : 32 * q + 32, :],
+                    out=outs[part][b, quarter * HC + h, g0 : g0 + 8, TG, :].rearrange(
+                        "g (x c) -> x g c", x=4
+                    ),
+                    in_=y[32 * q : 32 * q + 32, :],
                 )
 
         def make_add(s, r_tile, m_tile, blk):
@@ -163,55 +177,64 @@ def tile_causalselfattention2_pa_kernel(
                 m = m_tile[:].rearrange("p h j (i e) -> p (h j i) e", e=2)
                 nc.vector.tensor_tensor(out=r, in0=r, in1=m[:, :, ::-1], op=ADD)
                 for h in range(HB * blk, HB * blk + HB):
-                    store_rows(nc.gpsimd, s, r_tile, h, 0, J)
+                    store_rows(nc.sync, s, r_tile, h, 0, J)
 
             return run
 
         def push_mean(s, r_tile):
             state = {}
+            rotated = order[s][0] < 2
+            eng = nc.vector if rotated else nc.gpsimd
 
             def sum_a():
-                t = sums.tile([P, HC, 2 * HS], F32, name="pair_sums")
-                state["t"] = t
+                state["t"] = sums.tile([P, HC, 2 * HS], F32, name="pair_sums")
+                state["u"] = sums.tile([P, CHUNK], F32, align_bytes=64, name="four_sums")
+                state["q"] = sums.tile([P, TG // J, HS], F32, name="quarters")
                 r = r_tile[:].rearrange("p h j c -> p h (j c)")
-                nc.vector.tensor_tensor(
-                    out=t[:], in0=r[:, :, 0 : 2 * HS], in1=r[:, :, 2 * HS : 4 * HS], op=ADD
-                )
+                for h0 in range(0, HC, HC if rotated else HB):
+                    h1 = h0 + (HC if rotated else HB)
+                    eng.tensor_tensor(
+                        out=state["t"][:, h0:h1],
+                        in0=r[:, h0:h1, 0 : 2 * HS],
+                        in1=r[:, h0:h1, 2 * HS : 4 * HS],
+                        op=ADD,
+                    )
 
             def sum_b():
-                u = sums.tile([P, CHUNK], F32, align_bytes=64, name="four_sums")
-                t = state["t"]
-                state["u"] = u
-                nc.vector.tensor_tensor(
+                t, u, q = state["t"], state["u"], state["q"]
+                eng.tensor_tensor(
                     out=u[:].rearrange("p (h c) -> p h c", h=HC),
                     in0=t[:, :, 0:HS],
                     in1=t[:, :, HS : 2 * HS],
                     op=ADD,
                 )
+                for h in range(HC):
+                    for b in range(B):
+                        p0 = 64 * b + 16 * h
+                        nc.sync.dma_start(
+                            out=q[p0 : p0 + 16, :, :],
+                            in_=u[64 * b : 64 * b + 64, h * HS : h * HS + HS],
+                        )
 
-            def turn():
-                v = sums.tile([P, CHUNK], F32, align_bytes=64, name="turned")
-                nc.vector.transpose(out=v[:], in_=state["u"][:])
-                state["v"] = v
-
-            def reduce():
-                w = sums.tile([P, HS], F32, align_bytes=64, name="group_sums")
-                nc.vector.tensor_reduce(
-                    out=w[:].rearrange("p (m h g) -> p h m g", h=HC, g=8),
-                    in_=state["v"][:].rearrange("p (h m g r) -> p h m g r", h=HC, g=8, r=4),
-                    axis=AXIS_X,
-                    op=ADD,
-                )
-                state["w"] = w
-
-            def turn_back():
-                y = sums.tile([P, HS], F32, align_bytes=64, name="turned_back")
+            def sum_c():
+                q = state["q"]
+                w = sums.tile([P, 2, HS], F32, name="half_sums")
+                y = sums.tile([P, HS], F32, name="group_sums")
                 z = sums.tile([P, HS], F32, name="means")
-                nc.vector.transpose(out=y[:], in_=state["w"][:])
-                nc.scalar.activation(out=z[:], in_=y[:], func=COPY, scale=1.0 / TG)
-                store_means(nc.scalar, s, z)
+                nc.gpsimd.tensor_tensor(out=w[:], in0=q[:, 0:2], in1=q[:, 2:4], op=ADD)
+                nc.gpsimd.tensor_tensor(out=y[:], in0=w[:, 0], in1=w[:, 1], op=ADD)
+                nc.gpsimd.tensor_scalar(
+                    out=z[:], in0=y[:], scalar1=1.0 / TG, scalar2=0.0, op0=MULT, op1=ADD
+                )
 
-            pending.extend([sum_a, sum_b, turn, reduce, turn_back])
+                part, quarter = order[s]
+                for b in range(B):
+                    nc.gpsimd.dma_start(
+                        out=outs[part][b, quarter * HC : quarter * HC + HC, :, TG, :],
+                        in_=z[64 * b : 64 * b + 64, :],
+                    )
+
+            pending.extend([sum_a, sum_b, sum_c])
 
         def one_pass(acc, s, g, c0, c1, j):
             nc.tensor.matmul_mx(
@@ -273,24 +296,11 @@ def tile_causalselfattention2_pa_kernel(
                     pending.append(make_add(s, r_tile, m_tile, blk))
                 else:
                     for h in range(HB * blk, HB * blk + HB):
-                        store_rows(nc.gpsimd, s, r_tile, h, 0, J)
+                        store_rows(nc.sync, s, r_tile, h, 0, J)
             push_mean(s, r_tile)
 
         s = last
         r_tile = rows.tile([P, HC, J, HS], F32, name="r_tile")
-        w = sums.tile([P, HS], F32, align_bytes=64, name="group_sums")
-
-        def turn_and_reduce(u, h0, h1):
-            v = sums.tile([P, CHUNK], F32, align_bytes=64, name="turned")
-            n = (h1 - h0) * HS
-            nc.vector.transpose(out=v[:, 0:n], in_=u)
-            nc.vector.tensor_reduce(
-                out=w[:].rearrange("p (m h g) -> p h m g", h=HC, g=8)[:, h0:h1],
-                in_=v[:, 0:n].rearrange("p (h m g r) -> p h m g r", h=h1 - h0, g=8, r=4),
-                axis=AXIS_X,
-                op=ADD,
-            )
-
         def first_block_sums():
             t = sums.tile([P, HC, 2 * HS], F32, name="pair_sums")
             r = r_tile[:, 0:HB].rearrange("p h j c -> p h (j c)")
@@ -305,7 +315,8 @@ def tile_causalselfattention2_pa_kernel(
                 op=ADD,
             )
             nc.scalar.activation(out=u[:, NB : 2 * NB], in_=u[:, 0:NB], func=COPY, scale=1.0 / TG)
-            turn_and_reduce(u[:, NB : 2 * NB], 0, HB)
+            for h in range(HB):
+                head_means(nc.gpsimd, s, u[:, NB + h * HS : NB + h * HS + HS], h)
 
         for j in range(J):
             acc = psum.tile([P, NB], F32, name="acc")
@@ -334,8 +345,5 @@ def tile_causalselfattention2_pa_kernel(
                 nc.scalar.copy(out=r_tile[:, h, j, :], in_=bank)
                 if j == J - 2:
                     store_rows(nc.sync, s, r_tile, h, 0, J - 1)
-            turn_and_reduce(parts[:, J - 1], h, h + 1)
+            head_means(nc.gpsimd if h < HC - 1 else nc.scalar, s, parts[:, J - 1], h)
             store_rows(nc.sync, s, r_tile, h, J - 1, J)
-        y = sums.tile([P, HS], F32, align_bytes=64, name="turned_back")
-        nc.vector.transpose(out=y[:], in_=w[:])
-        store_means(nc.scalar, s, y)

@@ -43,6 +43,7 @@ def tile_causalselfattention2_pa_kernel(
         rows = ctx.enter_context(tc.tile_pool(name="rows", bufs=3))
         crossed = ctx.enter_context(tc.tile_pool(name="crossed", bufs=3))
         sums = ctx.enter_context(tc.tile_pool(name="sums", bufs=2))
+        tail = ctx.enter_context(tc.tile_pool(name="tail", bufs=4))
         psum = ctx.enter_context(tc.psum_pool(name="psum", bufs=8))
         ctx.enter_context(tc.manual_schedule())
 
@@ -57,6 +58,7 @@ def tile_causalselfattention2_pa_kernel(
         cos2 = keep.tile([P, J, HB, HS // 2, 2], BF16, name="cos2")
         sin2 = keep.tile([P, J, HB, HS // 2, 2], BF16, name="sin2")
 
+        warm = keep.tile([P, NB], BF16, name="warm")
         w_tiles = {}
 
         def col0(s):
@@ -80,35 +82,57 @@ def tile_causalselfattention2_pa_kernel(
                     in_=w_scales[:, r:16:4, c : c + CHUNK].rearrange("g q n -> q g n").bitcast(I32),
                 )
 
+        def load_first_w_scales(g0, g1):
+            for q in range(4):
+                nc.sync.dma_start(
+                    out=w_planes[0][32 * q : 32 * q + 4, g0:g1, :].bitcast(I32),
+                    in_=w_scales[g0:g1, 4 * q : 4 * q + 4, 0:CHUNK]
+                    .rearrange("g r n -> r g n")
+                    .bitcast(I32),
+                )
+
+        def load_x_scales(g0, g1):
+            for q in range(4):
+                nc.sync.dma_start(
+                    out=xs_raw[32 * q : 32 * q + 4, g0:g1, :].bitcast(I32),
+                    in_=x_scales[g0:g1, 4 * q : 4 * q + 4, :].rearrange("g r n -> r g n").bitcast(I32),
+                )
+
         def load_x_codes(g0, g1):
             nc.sync.dma_start(
                 out=x_raw[:, g0:g1, :], in_=x_words[g0:g1].rearrange("g p n -> p g n")
             )
 
-        nc.vector.memset(xs_raw[:].bitcast(I32), 0)
-        nc.gpsimd.memset(w_planes[0][:].bitcast(I32), 0)
+        nc.gpsimd.memset(warm[:], 0.0)
+        nc.vector.memset(xs_raw[:, 0:4, :].bitcast(I32), 0)
+        nc.vector.memset(w_planes[0][:, 0:4, :].bitcast(I32), 0)
+        nc.gpsimd.memset(xs_raw[:, 4:8, :].bitcast(I32), 0)
+        nc.gpsimd.memset(w_planes[0][:, 4:8, :].bitcast(I32), 0)
         load_x_codes(0, 1)
         load_w_codes(0, 0, 1)
-        for q in range(4):
-            nc.sync.dma_start(
-                out=xs_raw[32 * q : 32 * q + 4, :, :].bitcast(I32),
-                in_=x_scales[:, 4 * q : 4 * q + 4, :].rearrange("g r n -> r g n").bitcast(I32),
-            )
-        load_w_scales(0)
+        load_x_scales(0, 4)
+        load_first_w_scales(0, 4)
         load_x_codes(1, 2)
         load_w_codes(0, 1, 2)
         load_x_codes(2, 4)
         load_w_codes(0, 2, 4)
-        load_x_codes(4, 8)
-        load_w_codes(0, 4, 8)
+        load_x_scales(4, 8)
+        load_first_w_scales(4, 8)
+        load_x_codes(4, 6)
+        load_w_codes(0, 4, 6)
+        load_x_codes(6, 8)
+        load_w_codes(0, 6, 8)
+        warm_bank = psum.tile([P, NB], F32, name="acc")
+        for i in range(12):
+            nc.tensor.matmul(
+                out=warm_bank[:], lhsT=warm[:, 0:P], rhs=warm[:], start=True, stop=True
+            )
         for half in range(2):
             for i, f in enumerate((freqs_cos, freqs_sin)):
                 nc.gpsimd.dma_start(
                     out=cs_raw[64 * half : 64 * half + 64, i, :, :],
                     in_=f.rearrange("(p j) i -> p j i", j=J),
                 )
-        nc.gpsimd.memset(w_planes[1][:].bitcast(I32), 0)
-        nc.gpsimd.memset(w_planes[2][:].bitcast(I32), 0)
 
         for h in range(HB):
             for e in range(2):
@@ -131,6 +155,9 @@ def tile_causalselfattention2_pa_kernel(
         for g in range(PASSES):
             permute_x(g)
             permute_x_scales(g)
+            if g == 3:
+                nc.vector.memset(w_planes[1][:].bitcast(I32), 0)
+        nc.vector.memset(w_planes[2][:].bitcast(I32), 0)
 
         pending = []
 
@@ -148,11 +175,10 @@ def tile_causalselfattention2_pa_kernel(
                     in_=r_tile[64 * b : 64 * b + 64, h, j0:j1, :].rearrange("p j c -> p (j c)"),
                 )
 
-        def head_means(queue, s, u, h):
-            part, quarter = order[s]
-            v = sums.tile([P, HS], F32, align_bytes=64, name="turned")
-            w = sums.tile([P, HS // 4], F32, align_bytes=64, name="last_sums")
-            y = sums.tile([P, HS // 4], F32, align_bytes=64, name="turned_back")
+        def head_means(u):
+            v = tail.tile([P, HS], F32, align_bytes=64, name="turned")
+            w = tail.tile([P, HS // 4], F32, align_bytes=64, name="last_sums")
+            y = tail.tile([P, HS // 4], F32, align_bytes=64, name="turned_back")
             nc.vector.transpose(out=v[:], in_=u)
             nc.vector.tensor_reduce(
                 out=w[:].rearrange("p (m x g) -> p x m g", x=4, g=8),
@@ -162,9 +188,13 @@ def tile_causalselfattention2_pa_kernel(
             )
             for m in range(2):
                 nc.vector.transpose(out=y[:, 32 * m : 32 * m + 32], in_=w[:, 32 * m : 32 * m + 32])
+            return y
+
+        def store_head_means(s, y, h):
+            part, quarter = order[s]
             for q in range(4):
                 b, g0 = q // 2, 8 * (q % 2)
-                queue.dma_start(
+                nc.sync.dma_start(
                     out=outs[part][b, quarter * HC + h, g0 : g0 + 8, TG, :].rearrange(
                         "g (x c) -> x g c", x=4
                     ),
@@ -315,8 +345,7 @@ def tile_causalselfattention2_pa_kernel(
                 op=ADD,
             )
             nc.scalar.activation(out=u[:, NB : 2 * NB], in_=u[:, 0:NB], func=COPY, scale=1.0 / TG)
-            for h in range(HB):
-                head_means(nc.gpsimd, s, u[:, NB + h * HS : NB + h * HS + HS], h)
+            return [head_means(u[:, NB + h * HS : NB + h * HS + HS]) for h in range(HB)]
 
         for j in range(J):
             acc = psum.tile([P, NB], F32, name="acc")
@@ -328,7 +357,8 @@ def tile_causalselfattention2_pa_kernel(
             store_rows(nc.sync, s, r_tile, h, 0, J)
         while pending:
             pop()
-        first_block_sums()
+        head_tiles = first_block_sums()
+        stored = 0
         for h in range(HB, HC):
             parts = sums.tile([P, J, HS], F32, align_bytes=64, name="parts")
             for j in range(J):
@@ -345,5 +375,9 @@ def tile_causalselfattention2_pa_kernel(
                 nc.scalar.copy(out=r_tile[:, h, j, :], in_=bank)
                 if j == J - 2:
                     store_rows(nc.sync, s, r_tile, h, 0, J - 1)
-            head_means(nc.gpsimd if h < HC - 1 else nc.scalar, s, parts[:, J - 1], h)
+                    while len(head_tiles) > stored:
+                        store_head_means(s, head_tiles[stored], stored)
+                        stored += 1
             store_rows(nc.sync, s, r_tile, h, J - 1, J)
+            head_tiles.append(head_means(parts[:, J - 1]))
+        store_head_means(s, head_tiles[stored], stored)

@@ -41,9 +41,9 @@ def tile_causalselfattention2_pa_kernel(
         keep = ctx.enter_context(tc.tile_pool(name="keep", bufs=1))
         codes = ctx.enter_context(tc.tile_pool(name="codes", bufs=3))
         rows = ctx.enter_context(tc.tile_pool(name="rows", bufs=3))
-        crossed = ctx.enter_context(tc.tile_pool(name="crossed", bufs=3))
+        crossed = ctx.enter_context(tc.tile_pool(name="crossed", bufs=2))
         sums = ctx.enter_context(tc.tile_pool(name="sums", bufs=2))
-        tail = ctx.enter_context(tc.tile_pool(name="tail", bufs=4))
+        tail = ctx.enter_context(tc.tile_pool(name="tail", bufs=2))
         psum = ctx.enter_context(tc.psum_pool(name="psum", bufs=8))
         ctx.enter_context(tc.manual_schedule())
 
@@ -104,23 +104,23 @@ def tile_causalselfattention2_pa_kernel(
             )
 
         nc.gpsimd.memset(warm[:], 0.0)
-        nc.vector.memset(xs_raw[:, 0:4, :].bitcast(I32), 0)
-        nc.vector.memset(w_planes[0][:, 0:4, :].bitcast(I32), 0)
-        nc.gpsimd.memset(xs_raw[:, 4:8, :].bitcast(I32), 0)
-        nc.gpsimd.memset(w_planes[0][:, 4:8, :].bitcast(I32), 0)
+        nc.vector.memset(xs_raw[:, 0:3, :].bitcast(I32), 0)
+        nc.vector.memset(w_planes[0][:, 0:3, :].bitcast(I32), 0)
+        nc.gpsimd.memset(xs_raw[:, 3:8, :].bitcast(I32), 0)
+        nc.gpsimd.memset(w_planes[0][:, 3:8, :].bitcast(I32), 0)
+        nc.vector.memset(w_planes[1][:].bitcast(I32), 0)
         load_x_codes(0, 1)
         load_w_codes(0, 0, 1)
-        load_x_scales(0, 4)
-        load_first_w_scales(0, 4)
+        load_x_scales(0, 3)
+        load_first_w_scales(0, 3)
         load_x_codes(1, 2)
         load_w_codes(0, 1, 2)
-        load_x_codes(2, 4)
+        load_x_codes(2, 5)
         load_w_codes(0, 2, 4)
-        load_x_scales(4, 8)
-        load_first_w_scales(4, 8)
-        load_x_codes(4, 6)
+        load_x_scales(3, 8)
+        load_first_w_scales(3, 8)
+        load_x_codes(5, 8)
         load_w_codes(0, 4, 6)
-        load_x_codes(6, 8)
         load_w_codes(0, 6, 8)
         warm_bank = psum.tile([P, NB], F32, name="acc")
         for i in range(12):
@@ -155,9 +155,8 @@ def tile_causalselfattention2_pa_kernel(
         for g in range(PASSES):
             permute_x(g)
             permute_x_scales(g)
-            if g == 3:
-                nc.vector.memset(w_planes[1][:].bitcast(I32), 0)
-        nc.vector.memset(w_planes[2][:].bitcast(I32), 0)
+            if g == 5:
+                nc.vector.memset(w_planes[2][:].bitcast(I32), 0)
 
         pending = []
 
@@ -175,10 +174,10 @@ def tile_causalselfattention2_pa_kernel(
                     in_=r_tile[64 * b : 64 * b + 64, h, j0:j1, :].rearrange("p j c -> p (j c)"),
                 )
 
-        def head_means(u):
-            v = tail.tile([P, HS], F32, align_bytes=64, name="turned")
-            w = tail.tile([P, HS // 4], F32, align_bytes=64, name="last_sums")
-            y = tail.tile([P, HS // 4], F32, align_bytes=64, name="turned_back")
+        def block_means(u):
+            v = tail.tile([P, NB], F32, align_bytes=64, name="turned")
+            w = tail.tile([P, P], F32, align_bytes=64, name="last_sums")
+            y = tail.tile([P, P], F32, align_bytes=64, name="turned_back")
             nc.vector.transpose(out=v[:], in_=u)
             nc.vector.tensor_reduce(
                 out=w[:].rearrange("p (m x g) -> p x m g", x=4, g=8),
@@ -186,20 +185,19 @@ def tile_causalselfattention2_pa_kernel(
                 axis=AXIS_X,
                 op=ADD,
             )
-            for m in range(2):
-                nc.vector.transpose(out=y[:, 32 * m : 32 * m + 32], in_=w[:, 32 * m : 32 * m + 32])
+            nc.vector.transpose(out=y[:], in_=w[:])
             return y
 
-        def store_head_means(s, y, h):
+        def store_block_means(s, y, blk):
             part, quarter = order[s]
             for q in range(4):
                 b, g0 = q // 2, 8 * (q % 2)
-                nc.sync.dma_start(
-                    out=outs[part][b, quarter * HC + h, g0 : g0 + 8, TG, :].rearrange(
-                        "g (x c) -> x g c", x=4
-                    ),
-                    in_=y[32 * q : 32 * q + 32, :],
-                )
+                for i in range(HB):
+                    h = quarter * HC + HB * blk + i
+                    nc.sync.dma_start(
+                        out=outs[part][b, h, g0 : g0 + 8, TG, :].rearrange("g (x c) -> x g c", x=2),
+                        in_=y[32 * q + 16 * i : 32 * q + 16 * i + 16, :],
+                    )
 
         def make_add(s, r_tile, m_tile, blk):
             def run():
@@ -331,53 +329,44 @@ def tile_causalselfattention2_pa_kernel(
 
         s = last
         r_tile = rows.tile([P, HC, J, HS], F32, name="r_tile")
-        def first_block_sums():
-            t = sums.tile([P, HC, 2 * HS], F32, name="pair_sums")
-            r = r_tile[:, 0:HB].rearrange("p h j c -> p h (j c)")
-            nc.vector.tensor_tensor(
-                out=t[:, 0:HB], in0=r[:, :, 0 : 2 * HS], in1=r[:, :, 2 * HS : 4 * HS], op=ADD
-            )
-            u = sums.tile([P, CHUNK], F32, align_bytes=64, name="four_sums")
-            nc.vector.tensor_tensor(
-                out=u[:, 0:NB].rearrange("p (h c) -> p h c", h=HB),
-                in0=t[:, 0:HB, 0:HS],
-                in1=t[:, 0:HB, HS : 2 * HS],
-                op=ADD,
-            )
-            nc.scalar.activation(out=u[:, NB : 2 * NB], in_=u[:, 0:NB], func=COPY, scale=1.0 / TG)
-            return [head_means(u[:, NB + h * HS : NB + h * HS + HS]) for h in range(HB)]
-
-        for j in range(J):
-            acc = psum.tile([P, NB], F32, name="acc")
-            for g in range(PASSES):
-                one_pass(acc, s, g, 0, NB, j)
-            drain(s, acc, r_tile, None, 0, j)
-            pop()
-        for h in range(HB):
-            store_rows(nc.sync, s, r_tile, h, 0, J)
-        while pending:
-            pop()
-        head_tiles = first_block_sums()
-        stored = 0
-        for h in range(HB, HC):
-            parts = sums.tile([P, J, HS], F32, align_bytes=64, name="parts")
+        means = []
+        for blk in range(NBLK):
+            heads = range(HB * blk, HB * blk + HB)
+            parts = tail.tile([P, J, NB], F32, align_bytes=64, name="parts")
             for j in range(J):
-                acc = psum.tile([P, NB], F32, name="acc")
-                for g in range(PASSES):
-                    one_pass(acc, s, g, h * HS, h * HS + HS, j)
-                bank = acc[:, 0:HS]
-                if j == 0:
-                    nc.scalar.activation(out=parts[:, 0], in_=bank, func=COPY, scale=1.0 / TG)
-                else:
-                    nc.vector.scalar_tensor_tensor(
-                        out=parts[:, j], in0=bank, scalar=1.0 / TG, in1=parts[:, j - 1], op0=MULT, op1=ADD
+                step = HS if blk == NBLK - 1 and j == J - 1 else NB
+                for c0 in range(0, NB, step):
+                    acc = psum.tile([P, NB], F32, name="acc")
+                    for g in range(PASSES):
+                        one_pass(acc, s, g, blk * NB + c0, blk * NB + c0 + step, j)
+                    h0 = HB * blk + c0 // HS
+                    bank = acc[:, 0:step]
+                    nc.scalar.copy(
+                        out=r_tile[:, h0 : h0 + step // HS, j, :],
+                        in_=bank.rearrange("p (h c) -> p h c", c=HS),
                     )
-                nc.scalar.copy(out=r_tile[:, h, j, :], in_=bank)
+                    part_sum = parts[:, j, c0 : c0 + step]
+                    if j == 0:
+                        nc.scalar.activation(out=part_sum, in_=bank, func=COPY, scale=1.0 / TG)
+                    else:
+                        nc.vector.scalar_tensor_tensor(
+                            out=part_sum,
+                            in0=bank,
+                            scalar=1.0 / TG,
+                            in1=parts[:, j - 1, c0 : c0 + step],
+                            op0=MULT,
+                            op1=ADD,
+                        )
+                    if step == HS:
+                        store_rows(nc.sync, s, r_tile, h0, j, j + 1)
+                pop()
                 if j == J - 2:
-                    store_rows(nc.sync, s, r_tile, h, 0, J - 1)
-                    while len(head_tiles) > stored:
-                        store_head_means(s, head_tiles[stored], stored)
-                        stored += 1
-            store_rows(nc.sync, s, r_tile, h, J - 1, J)
-            head_tiles.append(head_means(parts[:, J - 1]))
-        store_head_means(s, head_tiles[stored], stored)
+                    for h in heads:
+                        store_rows(nc.sync, s, r_tile, h, 0, J - 1)
+                    if blk > 0:
+                        store_block_means(s, means[blk - 1], blk - 1)
+                if j == J - 1 and step == NB:
+                    for h in heads:
+                        store_rows(nc.sync, s, r_tile, h, j, j + 1)
+            means.append(block_means(parts[:, J - 1]))
+        store_block_means(s, means[-1], NBLK - 1)

@@ -104,26 +104,47 @@ def tile_causalselfattention2_pa_kernel(
             )
 
         nc.gpsimd.memset(warm[:], 0.0)
-        nc.vector.memset(xs_raw[:, 0:3, :].bitcast(I32), 0)
-        nc.vector.memset(w_planes[0][:, 0:3, :].bitcast(I32), 0)
-        nc.gpsimd.memset(xs_raw[:, 3:8, :].bitcast(I32), 0)
-        nc.gpsimd.memset(w_planes[0][:, 3:8, :].bitcast(I32), 0)
-        nc.vector.memset(w_planes[1][:].bitcast(I32), 0)
+        nc.vector.memset(xs_raw[:, 0:4, :].bitcast(I32), 0)
+        nc.vector.memset(w_planes[0][:, 0:4, :].bitcast(I32), 0)
         load_x_codes(0, 1)
         load_w_codes(0, 0, 1)
-        load_x_scales(0, 3)
-        load_first_w_scales(0, 3)
+        load_x_scales(0, 4)
+        load_first_w_scales(0, 4)
         load_x_codes(1, 2)
         load_w_codes(0, 1, 2)
-        load_x_codes(2, 5)
+        load_x_codes(2, 4)
         load_w_codes(0, 2, 4)
-        load_x_scales(3, 8)
-        load_first_w_scales(3, 8)
-        load_x_codes(5, 8)
+
+        def permute_x(g):
+            nc.vector.tensor_copy(
+                out=x_codes[:, g].rearrange("p j (m b) -> p j m b", b=2),
+                in_=x_raw[:, g].rearrange("p (m j b) -> p j m b", j=J, b=2),
+            )
+
+        def permute_x_scales(g):
+            nc.vector.tensor_copy(
+                out=x_planes[:, g], in_=xs_raw[:, g].rearrange("p (m j) -> p j m", j=J)
+            )
+
+        permute_x(0)
+        permute_x_scales(0)
+        nc.vector.memset(xs_raw[:, 4:8, :].bitcast(I32), 0)
+        nc.vector.memset(w_planes[0][:, 4:8, :].bitcast(I32), 0)
+        load_x_scales(4, 8)
+        load_first_w_scales(4, 8)
+        load_x_codes(4, 6)
         load_w_codes(0, 4, 6)
+        load_x_codes(6, 8)
         load_w_codes(0, 6, 8)
+        for g in range(1, PASSES):
+            permute_x(g)
+            permute_x_scales(g)
+            if g == 3:
+                nc.vector.memset(w_planes[1][:].bitcast(I32), 0)
+        nc.vector.memset(w_planes[2][:].bitcast(I32), 0)
+
         warm_bank = psum.tile([P, NB], F32, name="acc")
-        for i in range(12):
+        for i in range(14):
             nc.tensor.matmul(
                 out=warm_bank[:], lhsT=warm[:, 0:P], rhs=warm[:], start=True, stop=True
             )
@@ -140,23 +161,6 @@ def tile_causalselfattention2_pa_kernel(
                 nc.scalar.activation(
                     out=sin2[:, :, h, :, e], in_=cs_raw[:, 1], func=COPY, scale=1.0 - 2.0 * e
                 )
-
-        def permute_x(g):
-            nc.vector.tensor_copy(
-                out=x_codes[:, g].rearrange("p j (m b) -> p j m b", b=2),
-                in_=x_raw[:, g].rearrange("p (m j b) -> p j m b", j=J, b=2),
-            )
-
-        def permute_x_scales(g):
-            nc.vector.tensor_copy(
-                out=x_planes[:, g], in_=xs_raw[:, g].rearrange("p (m j) -> p j m", j=J)
-            )
-
-        for g in range(PASSES):
-            permute_x(g)
-            permute_x_scales(g)
-            if g == 5:
-                nc.vector.memset(w_planes[2][:].bitcast(I32), 0)
 
         pending = []
 

from contextlib import ExitStack

import concourse.mybir as mybir

B, T, C, H = 2, 256, 4096, 16
G = 16
TG = T // G
HS = C // H
TOK = B * T

F32 = mybir.dt.float32
BF16 = mybir.dt.bfloat16
I32 = mybir.dt.int32
U8 = mybir.dt.uint8
FP4X4 = mybir.dt.float4_e2m1fn_x4
ADD = mybir.AluOpType.add
MULT = mybir.AluOpType.mult
COPY = mybir.ActivationFunctionType.Copy
AXIS_X = mybir.AxisListType.X

FLOPS = 2 * TOK * C * 3 * C

P = 128
PASSES = C // 512
J = TOK // P
NB = 512
CHUNK = 1024
NBLK = CHUNK // NB
HC = CHUNK // HS
HB = NB // HS


def tile_causalselfattention2_pa_kernel(
    tc, x_words, x_scales, w_words, w_scales, freqs_cos, freqs_sin, out_q, out_k, out_v
):
    nc = tc.nc
    outs = [out_q, out_k, out_v]
    order = [(part, quarter) for quarter in range(C // CHUNK) for part in range(3)]

    with ExitStack() as ctx:
        keep = ctx.enter_context(tc.tile_pool(name="keep", bufs=1))
        codes = ctx.enter_context(tc.tile_pool(name="codes", bufs=3))
        rows = ctx.enter_context(tc.tile_pool(name="rows", bufs=3))
        crossed = ctx.enter_context(tc.tile_pool(name="crossed", bufs=2))
        sums = ctx.enter_context(tc.tile_pool(name="sums", bufs=2))
        tail = ctx.enter_context(tc.tile_pool(name="tail", bufs=2))
        psum = ctx.enter_context(tc.psum_pool(name="psum", bufs=8))
        ctx.enter_context(tc.manual_schedule())

        x_raw = keep.tile([P, PASSES, 2 * TOK], U8, align_bytes=64, name="x_raw")
        xs_raw = keep.tile([P, PASSES, TOK], U8, align_bytes=64, name="xs_raw")
        x_codes = keep.tile([P, PASSES, J, 2 * P], U8, align_bytes=64, name="x_codes")
        x_planes = keep.tile([P, PASSES, J, P], U8, align_bytes=64, name="x_planes")
        w_planes = [
            keep.tile([P, PASSES, CHUNK], U8, align_bytes=64, name="w_planes%d" % i) for i in range(3)
        ]
        cs_raw = keep.tile([P, 2, J, HS // 2], BF16, name="cs_raw")
        cos2 = keep.tile([P, J, HB, HS // 2, 2], BF16, name="cos2")
        sin2 = keep.tile([P, J, HB, HS // 2, 2], BF16, name="sin2")

        warm = keep.tile([P, NB], BF16, name="warm")
        w_tiles = {}

        def col0(s):
            part, quarter = order[s]
            return part * C + quarter * CHUNK

        def load_w_codes(s, g0, g1):
            if s not in w_tiles:
                w_tiles[s] = codes.tile([P, PASSES, 2 * CHUNK], U8, align_bytes=64, name="w_codes")
            c = col0(s)
            nc.sync.dma_start(
                out=w_tiles[s][:, g0:g1, :],
                in_=w_words[g0:g1, :, 2 * c : 2 * (c + CHUNK)].rearrange("g p n -> p g n"),
            )

        def load_w_scales(s):
            c = col0(s)
            for r in range(4):
                nc.sync.dma_start(
                    out=w_planes[s % 3][r:P:32, :, :].bitcast(I32),
                    in_=w_scales[:, r:16:4, c : c + CHUNK].rearrange("g q n -> q g n").bitcast(I32),
                )

        def load_first_w_scales(g0, g1):
            for q in range(4):
                nc.sync.dma_start(
                    out=w_planes[0][32 * q : 32 * q + 4, g0:g1, :].bitcast(I32),
                    in_=w_scales[g0:g1, 4 * q : 4 * q + 4, 0:CHUNK]
                    .rearrange("g r n -> r g n")
                    .bitcast(I32),
                )

        def load_x_scales(g0, g1):
            for q in range(4):
                nc.sync.dma_start(
                    out=xs_raw[32 * q : 32 * q + 4, g0:g1, :].bitcast(I32),
                    in_=x_scales[g0:g1, 4 * q : 4 * q + 4, :].rearrange("g r n -> r g n").bitcast(I32),
                )

        def load_x_codes(g0, g1):
            nc.sync.dma_start(
                out=x_raw[:, g0:g1, :], in_=x_words[g0:g1].rearrange("g p n -> p g n")
            )

        nc.gpsimd.memset(warm[:], 0.0)
        nc.vector.memset(xs_raw[:, 0:4, :].bitcast(I32), 0)
        nc.vector.memset(w_planes[0][:, 0:4, :].bitcast(I32), 0)
        load_x_codes(0, 1)
        load_w_codes(0, 0, 1)
        load_x_scales(0, 4)
        load_first_w_scales(0, 4)
        load_x_codes(1, 2)
        load_w_codes(0, 1, 2)
        load_x_codes(2, 4)
        load_w_codes(0, 2, 4)

        def permute_x(g):
            nc.vector.tensor_copy(
                out=x_codes[:, g].rearrange("p j (m b) -> p j m b", b=2),
                in_=x_raw[:, g].rearrange("p (m j b) -> p j m b", j=J, b=2),
            )

        def permute_x_scales(g):
            nc.vector.tensor_copy(
                out=x_planes[:, g], in_=xs_raw[:, g].rearrange("p (m j) -> p j m", j=J)
            )

        permute_x(0)
        permute_x_scales(0)
        nc.vector.memset(xs_raw[:, 4:8, :].bitcast(I32), 0)
        nc.vector.memset(w_planes[0][:, 4:8, :].bitcast(I32), 0)
        load_x_scales(4, 8)
        load_first_w_scales(4, 8)
        load_x_codes(4, 6)
        load_w_codes(0, 4, 6)
        load_x_codes(6, 8)
        load_w_codes(0, 6, 8)
        for g in range(1, PASSES):
            permute_x(g)
            permute_x_scales(g)
            if g == 3:
                nc.vector.memset(w_planes[1][:].bitcast(I32), 0)
        nc.vector.memset(w_planes[2][:].bitcast(I32), 0)

        warm_bank = psum.tile([P, NB], F32, name="acc")
        for i in range(14):
            nc.tensor.matmul(
                out=warm_bank[:], lhsT=warm[:, 0:P], rhs=warm[:], start=True, stop=True
            )
        for half in range(2):
            for i, f in enumerate((freqs_cos, freqs_sin)):
                nc.gpsimd.dma_start(
                    out=cs_raw[64 * half : 64 * half + 64, i, :, :],
                    in_=f.rearrange("(p j) i -> p j i", j=J),
                )

        for h in range(HB):
            for e in range(2):
                nc.scalar.activation(out=cos2[:, :, h, :, e], in_=cs_raw[:, 0], func=COPY)
                nc.scalar.activation(
                    out=sin2[:, :, h, :, e], in_=cs_raw[:, 1], func=COPY, scale=1.0 - 2.0 * e
                )

        pending = []

        def pop():
            if pending:
                pending.pop(0)()

        def store_rows(queue, s, r_tile, h, j0, j1):
            part, quarter = order[s]
            for b in range(B):
                queue.dma_start(
                    out=outs[part][b, quarter * HC + h, :, 0:TG, :].rearrange(
                        "g (r j) c -> g r (j c)", j=J
                    )[:, :, j0 * HS : j1 * HS],
                    in_=r_tile[64 * b : 64 * b + 64, h, j0:j1, :].rearrange("p j c -> p (j c)"),
                )

        def block_means(u):
            v = tail.tile([P, NB], F32, align_bytes=64, name="turned")
            w = tail.tile([P, P], F32, align_bytes=64, name="last_sums")
            y = tail.tile([P, P], F32, align_bytes=64, name="turned_back")
            nc.vector.transpose(out=v[:], in_=u)
            nc.vector.tensor_reduce(
                out=w[:].rearrange("p (m x g) -> p x m g", x=4, g=8),
                in_=v[:].rearrange("p (x m g r) -> p x m g r", x=4, g=8, r=4),
                axis=AXIS_X,
                op=ADD,
            )
            nc.vector.transpose(out=y[:], in_=w[:])
            return y

        def store_block_means(s, y, blk):
            part, quarter = order[s]
            for q in range(4):
                b, g0 = q // 2, 8 * (q % 2)
                for i in range(HB):
                    h = quarter * HC + HB * blk + i
                    nc.sync.dma_start(
                        out=outs[part][b, h, g0 : g0 + 8, TG, :].rearrange("g (x c) -> x g c", x=2),
                        in_=y[32 * q + 16 * i : 32 * q + 16 * i + 16, :],
                    )

        def make_add(s, r_tile, m_tile, blk):
            def run():
                r = r_tile[:, HB * blk : HB * blk + HB].rearrange("p h j (i e) -> p (h j i) e", e=2)
                m = m_tile[:].rearrange("p h j (i e) -> p (h j i) e", e=2)
                nc.vector.tensor_tensor(out=r, in0=r, in1=m[:, :, ::-1], op=ADD)
                for h in range(HB * blk, HB * blk + HB):
                    store_rows(nc.sync, s, r_tile, h, 0, J)

            return run

        def push_mean(s, r_tile):
            state = {}
            rotated = order[s][0] < 2
            eng = nc.vector if rotated else nc.gpsimd

            def sum_a():
                state["t"] = sums.tile([P, HC, 2 * HS], F32, name="pair_sums")
                state["u"] = sums.tile([P, CHUNK], F32, align_bytes=64, name="four_sums")
                state["q"] = sums.tile([P, TG // J, HS], F32, name="quarters")
                r = r_tile[:].rearrange("p h j c -> p h (j c)")
                for h0 in range(0, HC, HC if rotated else HB):
                    h1 = h0 + (HC if rotated else HB)
                    eng.tensor_tensor(
                        out=state["t"][:, h0:h1],
                        in0=r[:, h0:h1, 0 : 2 * HS],
                        in1=r[:, h0:h1, 2 * HS : 4 * HS],
                        op=ADD,
                    )

            def sum_b():
                t, u, q = state["t"], state["u"], state["q"]
                eng.tensor_tensor(
                    out=u[:].rearrange("p (h c) -> p h c", h=HC),
                    in0=t[:, :, 0:HS],
                    in1=t[:, :, HS : 2 * HS],
                    op=ADD,
                )
                for h in range(HC):
                    for b in range(B):
                        p0 = 64 * b + 16 * h
                        nc.sync.dma_start(
                            out=q[p0 : p0 + 16, :, :],
                            in_=u[64 * b : 64 * b + 64, h * HS : h * HS + HS],
                        )

            def sum_c():
                q = state["q"]
                w = sums.tile([P, 2, HS], F32, name="half_sums")
                y = sums.tile([P, HS], F32, name="group_sums")
                z = sums.tile([P, HS], F32, name="means")
                nc.gpsimd.tensor_tensor(out=w[:], in0=q[:, 0:2], in1=q[:, 2:4], op=ADD)
                nc.gpsimd.tensor_tensor(out=y[:], in0=w[:, 0], in1=w[:, 1], op=ADD)
                nc.gpsimd.tensor_scalar(
                    out=z[:], in0=y[:], scalar1=1.0 / TG, scalar2=0.0, op0=MULT, op1=ADD
                )

                part, quarter = order[s]
                for b in range(B):
                    nc.gpsimd.dma_start(
                        out=outs[part][b, quarter * HC : quarter * HC + HC, :, TG, :],
                        in_=z[64 * b : 64 * b + 64, :],
                    )

            pending.extend([sum_a, sum_b, sum_c])

        def one_pass(acc, s, g, c0, c1, j):
            nc.tensor.matmul_mx(
                out=acc[:, 0 : c1 - c0],
                lhsT=x_codes[:, g, j, :].bitcast(FP4X4),
                lhsT_scale=x_planes[:, g, j, :],
                rhs=w_tiles[s][:, g, 2 * c0 : 2 * c1].bitcast(FP4X4),
                rhs_scale=w_planes[s % 3][:, g, c0:c1],
                start=(g == 0),
                stop=(g == PASSES - 1),
            )

        def drain(s, acc, r_tile, m_tile, blk, j):
            bank = acc[:].rearrange("p (h c) -> p h c", h=HB)
            out = r_tile[:, HB * blk : HB * blk + HB, j, :]
            if order[s][0] == 2:
                nc.scalar.copy(out=out, in_=bank)
            else:
                nc.vector.tensor_tensor(
                    out=out, in0=bank, in1=cos2[:, j].rearrange("p h i e -> p h (i e)"), op=MULT
                )
                nc.vector.tensor_tensor(
                    out=m_tile[:, :, j, :],
                    in0=bank,
                    in1=sin2[:, j].rearrange("p h i e -> p h (i e)"),
                    op=MULT,
                )
            pop()

        def load_chunk(s):
            if s < len(order):
                load_w_scales(s)
                load_w_codes(s, 0, 4)
                load_w_codes(s, 4, 8)

        load_chunk(1)
        last = len(order) - 1
        for s in range(last):
            load_chunk(s + 2)
            rotated = order[s][0] < 2
            r_tile = rows.tile([P, HC, J, HS], F32, name="r_tile")
            accs = {}
            if s == 0:
                for g in range(PASSES):
                    for blk in range(NBLK):
                        for j in range(J):
                            if g == 0:
                                accs[blk, j] = psum.tile([P, NB], F32, name="acc")
                            one_pass(accs[blk, j], s, g, blk * NB, blk * NB + NB, j)
            for blk in range(NBLK):
                m_tile = crossed.tile([P, HB, J, HS], F32, name="m_tile") if rotated else None
                for j in range(J):
                    if s > 0:
                        accs[blk, j] = psum.tile([P, NB], F32, name="acc")
                        for g in range(PASSES):
                            one_pass(accs[blk, j], s, g, blk * NB, blk * NB + NB, j)
                    drain(s, accs[blk, j], r_tile, m_tile, blk, j)
                if rotated:
                    pending.append(make_add(s, r_tile, m_tile, blk))
                else:
                    for h in range(HB * blk, HB * blk + HB):
                        store_rows(nc.sync, s, r_tile, h, 0, J)
            push_mean(s, r_tile)

        s = last
        r_tile = rows.tile([P, HC, J, HS], F32, name="r_tile")
        means = []
        for blk in range(NBLK):
            heads = range(HB * blk, HB * blk + HB)
            parts = tail.tile([P, J, NB], F32, align_bytes=64, name="parts")
            for j in range(J):
                step = HS if blk == NBLK - 1 and j == J - 1 else NB
                for c0 in range(0, NB, step):
                    acc = psum.tile([P, NB], F32, name="acc")
                    for g in range(PASSES):
                        one_pass(acc, s, g, blk * NB + c0, blk * NB + c0 + step, j)
                    h0 = HB * blk + c0 // HS
                    bank = acc[:, 0:step]
                    nc.scalar.copy(
                        out=r_tile[:, h0 : h0 + step // HS, j, :],
                        in_=bank.rearrange("p (h c) -> p h c", c=HS),
                    )
                    part_sum = parts[:, j, c0 : c0 + step]
                    if j == 0:
                        nc.scalar.activation(out=part_sum, in_=bank, func=COPY, scale=1.0 / TG)
                    else:
                        nc.vector.scalar_tensor_tensor(
                            out=part_sum,
                            in0=bank,
                            scalar=1.0 / TG,
                            in1=parts[:, j - 1, c0 : c0 + step],
                            op0=MULT,
                            op1=ADD,
                        )
                    if step == HS:
                        store_rows(nc.sync, s, r_tile, h0, j, j + 1)
                pop()
                if j == J - 2:
                    for h in heads:
                        store_rows(nc.sync, s, r_tile, h, 0, J - 1)
                    if blk > 0:
                        store_block_means(s, means[blk - 1], blk - 1)
                if j == J - 1 and step == NB:
                    for h in heads:
                        store_rows(nc.sync, s, r_tile, h, j, j + 1)
            means.append(block_means(parts[:, J - 1]))
        store_block_means(s, means[-1], NBLK - 1)
